import numpy as np
import ml_dtypes

BF16 = ml_dtypes.bfloat16


def bf(x):
    return np.asarray(x, np.float32).astype(BF16)


def f32(x):
    return np.asarray(x, np.float32)


def f64(x):
    return np.asarray(x).astype(np.float64)


def striped(idx):
    return np.tile(idx.reshape(-1, 16).T, (8, 1))


C, S, N, K = 512, 1024, 512, 3


def setup_inputs():
    return {"emb": f32(np.random.standard_normal((C, S))), "cons": f32(np.random.uniform(size=(1, N))), "cons_w": f32(np.random.standard_normal((C, 1))), "cons_b": f32(0.1 * np.random.standard_normal((C, 1))), "state": f32(np.random.standard_normal((1, K))), "state_w": f32(np.random.standard_normal((C, K)) / np.sqrt(K)), "state_b": f32(0.1 * np.random.standard_normal((C, 1))), "offs": striped(np.random.permutation(np.tile(np.arange(S), 2))[:N])}


def reference(emb, cons, cons_w, cons_b, state, state_w, state_b, offs):
    idx = offs[:16].T.reshape(-1)
    state_term = (f64(state_w) * f64(state)).sum(axis=1, keepdims=True) + f64(state_b)
    other = f64(cons_w) * f64(cons) + f64(cons_b) + state_term
    return f64(emb)[:, idx] + other

@@ -1,0 +1,61 @@
+import concourse.mybir as mybir
+
+F32 = mybir.dt.float32
+U16 = mybir.dt.uint16
+ADD = mybir.AluOpType.add
+MULT = mybir.AluOpType.mult
+IDENTITY = mybir.ActivationFunctionType.Identity
+
+P = 128
+C, S, N, K = 512, 1024, 512, 3
+B = C // P
+
+
+def tile_allostericmessagepassingencoder_kernel(
+    tc, emb, cons, cons_w, cons_b, state, state_w, state_b, offs, out
+):
+    nc = tc.nc
+
+    emb_blocks = emb.rearrange("(p b) s -> b p s", b=B)
+    out_blocks = out.rearrange("(p b) n -> b p n", b=B)
+
+    with tc.tile_pool(name="held", bufs=1) as held:
+        offsets = held.tile([P, N // 16], U16, name="offsets")
+        nc.sync.dma_start(offsets[:], offs)
+
+        state_w_sb = held.tile([P, B, K], F32, name="state_w_sb")
+        nc.scalar.dma_start(state_w_sb[:], state_w.rearrange("(p b) k -> p b k", b=B))
+        state_sb = held.tile([P, K], F32, name="state_sb")
+        nc.scalar.dma_start(state_sb[:], state.rearrange("o k -> (o k)").partition_broadcast(P))
+        cons_sb = held.tile([P, N], F32, name="cons_sb")
+        nc.scalar.dma_start(cons_sb[:], cons.rearrange("o n -> (o n)").partition_broadcast(P))
+        cons_b_sb = held.tile([P, B], F32, name="cons_b_sb")
+        nc.gpsimd.dma_start(cons_b_sb[:], cons_b.rearrange("(p b) o -> p (b o)", b=B))
+        state_b_sb = held.tile([P, B], F32, name="state_b_sb")
+        nc.gpsimd.dma_start(state_b_sb[:], state_b.rearrange("(p b) o -> p (b o)", b=B))
+        cons_w_sb = held.tile([P, B], F32, name="cons_w_sb")
+        nc.gpsimd.dma_start(cons_w_sb[:], cons_w.rearrange("(p b) o -> p (b o)", b=B))
+
+        windows = []
+        for b in range(B):
+            window = held.tile([P, S], F32, name=f"window{b}")
+            nc.sync.dma_start(window[:], emb_blocks[b])
+            windows.append(window)
+
+        products = held.tile([P, B, K], F32, name="products")
+        nc.vector.tensor_tensor(
+            products[:], state_w_sb[:], state_sb[:].unsqueeze(1).to_broadcast([P, B, K]), MULT
+        )
+        bias = held.tile([P, B], F32, name="bias")
+        nc.vector.tensor_reduce(bias[:], products[:], axis=mybir.AxisListType.X, op=ADD)
+        nc.vector.tensor_tensor(bias[:], bias[:], cons_b_sb[:], ADD)
+        nc.vector.tensor_tensor(bias[:], bias[:], state_b_sb[:], ADD)
+
+        for b in range(B):
+            other = held.tile([P, N], F32, name=f"other{b}")
+            nc.scalar.activation(
+                other[:], cons_sb[:], IDENTITY, bias=bias[:, b : b + 1], scale=cons_w_sb[:, b : b + 1]
+            )
+            result = held.tile([P, N], F32, name=f"result{b}")
+            nc.vector.tensor_tensor(result[:], windows[b][:].indirect(offsets[:]), other[:], ADD)
+            nc.sync.dma_start(out_blocks[b], result[:])

@@ -30,11 +30,11 @@ def tile_allostericmessagepassingencoder_kernel(
         cons_sb = held.tile([P, N], F32, name="cons_sb")
         nc.scalar.dma_start(cons_sb[:], cons.rearrange("o n -> (o n)").partition_broadcast(P))
         cons_b_sb = held.tile([P, B], F32, name="cons_b_sb")
-        nc.gpsimd.dma_start(cons_b_sb[:], cons_b.rearrange("(p b) o -> p (b o)", b=B))
+        nc.scalar.dma_start(cons_b_sb[:], cons_b.rearrange("(p b) o -> p (b o)", b=B))
         state_b_sb = held.tile([P, B], F32, name="state_b_sb")
-        nc.gpsimd.dma_start(state_b_sb[:], state_b.rearrange("(p b) o -> p (b o)", b=B))
+        nc.scalar.dma_start(state_b_sb[:], state_b.rearrange("(p b) o -> p (b o)", b=B))
         cons_w_sb = held.tile([P, B], F32, name="cons_w_sb")
-        nc.gpsimd.dma_start(cons_w_sb[:], cons_w.rearrange("(p b) o -> p (b o)", b=B))
+        nc.scalar.dma_start(cons_w_sb[:], cons_w.rearrange("(p b) o -> p (b o)", b=B))
 
         windows = []
         for b in range(B):

@@ -4,7 +4,6 @@ F32 = mybir.dt.float32
 U16 = mybir.dt.uint16
 ADD = mybir.AluOpType.add
 MULT = mybir.AluOpType.mult
-IDENTITY = mybir.ActivationFunctionType.Identity
 
 P = 128
 C, S, N, K = 512, 1024, 512, 3
@@ -53,8 +52,8 @@ def tile_allostericmessagepassingencoder_kernel(
 
         for b in range(B):
             other = held.tile([P, N], F32, name=f"other{b}")
-            nc.scalar.activation(
-                other[:], cons_sb[:], IDENTITY, bias=bias[:, b : b + 1], scale=cons_w_sb[:, b : b + 1]
+            nc.vector.tensor_scalar(
+                other[:], cons_sb[:], cons_w_sb[:, b : b + 1], bias[:, b : b + 1], MULT, ADD
             )
             result = held.tile([P, N], F32, name=f"result{b}")
             nc.vector.tensor_tensor(result[:], windows[b][:].indirect(offsets[:]), other[:], ADD)

@@ -20,26 +20,24 @@ def tile_allostericmessagepassingencoder_kernel(
 
     with tc.tile_pool(name="held", bufs=1) as held:
         offsets = held.tile([P, N // 16], U16, name="offsets")
-        nc.sync.dma_start(offsets[:], offs)
-
         state_w_sb = held.tile([P, B, K], F32, name="state_w_sb")
-        nc.scalar.dma_start(state_w_sb[:], state_w.rearrange("(p b) k -> p b k", b=B))
         state_sb = held.tile([P, K], F32, name="state_sb")
-        nc.scalar.dma_start(state_sb[:], state.rearrange("o k -> (o k)").partition_broadcast(P))
         cons_sb = held.tile([P, N], F32, name="cons_sb")
-        nc.scalar.dma_start(cons_sb[:], cons.rearrange("o n -> (o n)").partition_broadcast(P))
         cons_b_sb = held.tile([P, B], F32, name="cons_b_sb")
-        nc.scalar.dma_start(cons_b_sb[:], cons_b.rearrange("(p b) o -> p (b o)", b=B))
         state_b_sb = held.tile([P, B], F32, name="state_b_sb")
-        nc.scalar.dma_start(state_b_sb[:], state_b.rearrange("(p b) o -> p (b o)", b=B))
         cons_w_sb = held.tile([P, B], F32, name="cons_w_sb")
-        nc.scalar.dma_start(cons_w_sb[:], cons_w.rearrange("(p b) o -> p (b o)", b=B))
+        windows = [held.tile([P, S], F32, name=f"window{b}") for b in range(B)]
 
-        windows = []
-        for b in range(B):
-            window = held.tile([P, S], F32, name=f"window{b}")
-            nc.sync.dma_start(window[:], emb_blocks[b])
-            windows.append(window)
+        nc.scalar.dma_start(windows[0][:], emb_blocks[0])
+        nc.sync.dma_start(state_w_sb[:], state_w.rearrange("(p b) k -> p b k", b=B))
+        nc.scalar.dma_start(state_sb[:], state.rearrange("o k -> (o k)").partition_broadcast(P))
+        nc.sync.dma_start(cons_b_sb[:], cons_b.rearrange("(p b) o -> p (b o)", b=B))
+        nc.scalar.dma_start(state_b_sb[:], state_b.rearrange("(p b) o -> p (b o)", b=B))
+        nc.sync.dma_start(cons_sb[:], cons.rearrange("o n -> (o n)").partition_broadcast(P))
+        nc.scalar.dma_start(cons_w_sb[:], cons_w.rearrange("(p b) o -> p (b o)", b=B))
+        nc.sync.dma_start(offsets[:], offs)
+        for b in range(1, B):
+            nc.sync.dma_start(windows[b][:], emb_blocks[b])
 
         products = held.tile([P, B, K], F32, name="products")
         nc.vector.tensor_tensor(

@@ -28,15 +28,14 @@ def tile_allostericmessagepassingencoder_kernel(
         cons_w_sb = held.tile([P, B], F32, name="cons_w_sb")
         windows = [held.tile([P, S], F32, name=f"window{b}") for b in range(B)]
 
-        nc.scalar.dma_start(windows[0][:], emb_blocks[0])
         nc.sync.dma_start(state_w_sb[:], state_w.rearrange("(p b) k -> p b k", b=B))
         nc.scalar.dma_start(state_sb[:], state.rearrange("o k -> (o k)").partition_broadcast(P))
         nc.sync.dma_start(cons_b_sb[:], cons_b.rearrange("(p b) o -> p (b o)", b=B))
         nc.scalar.dma_start(state_b_sb[:], state_b.rearrange("(p b) o -> p (b o)", b=B))
-        nc.sync.dma_start(cons_sb[:], cons.rearrange("o n -> (o n)").partition_broadcast(P))
-        nc.scalar.dma_start(cons_w_sb[:], cons_w.rearrange("(p b) o -> p (b o)", b=B))
+        nc.sync.dma_start(cons_w_sb[:], cons_w.rearrange("(p b) o -> p (b o)", b=B))
+        nc.scalar.dma_start(cons_sb[:], cons.rearrange("o n -> (o n)").partition_broadcast(P))
         nc.sync.dma_start(offsets[:], offs)
-        for b in range(1, B):
+        for b in range(B):
             nc.sync.dma_start(windows[b][:], emb_blocks[b])
 
         products = held.tile([P, B, K], F32, name="products")
@@ -48,11 +47,15 @@ def tile_allostericmessagepassingencoder_kernel(
         nc.vector.tensor_tensor(bias[:], bias[:], cons_b_sb[:], ADD)
         nc.vector.tensor_tensor(bias[:], bias[:], state_b_sb[:], ADD)
 
+        others = []
         for b in range(B):
             other = held.tile([P, N], F32, name=f"other{b}")
             nc.vector.tensor_scalar(
                 other[:], cons_sb[:], cons_w_sb[:, b : b + 1], bias[:, b : b + 1], MULT, ADD
             )
+            others.append(other)
+
+        for b in range(B):
             result = held.tile([P, N], F32, name=f"result{b}")
-            nc.vector.tensor_tensor(result[:], windows[b][:].indirect(offsets[:]), other[:], ADD)
+            nc.vector.tensor_tensor(result[:], windows[b][:].indirect(offsets[:]), others[b][:], ADD)
             nc.sync.dma_start(out_blocks[b], result[:])

@@ -57,5 +57,13 @@ def tile_allostericmessagepassingencoder_kernel(
 
         for b in range(B):
             result = held.tile([P, N], F32, name=f"result{b}")
-            nc.vector.tensor_tensor(result[:], windows[b][:].indirect(offsets[:]), others[b][:], ADD)
-            nc.sync.dma_start(out_blocks[b], result[:])
+            pieces = 2 if b == B - 1 else 1
+            n = N // pieces
+            for j in range(0, N, n):
+                nc.vector.tensor_tensor(
+                    result[:, j : j + n],
+                    windows[b][:].indirect(offsets[:, j // 16 : (j + n) // 16]),
+                    others[b][:, j : j + n],
+                    ADD,
+                )
+                nc.sync.dma_start(out_blocks[b][:, j : j + n], result[:, j : j + n])

@@ -23,29 +23,30 @@ def tile_allostericmessagepassingencoder_kernel(
         state_w_sb = held.tile([P, B, K], F32, name="state_w_sb")
         state_sb = held.tile([P, K], F32, name="state_sb")
         cons_sb = held.tile([P, N], F32, name="cons_sb")
-        cons_b_sb = held.tile([P, B], F32, name="cons_b_sb")
-        state_b_sb = held.tile([P, B], F32, name="state_b_sb")
+        terms = held.tile([P, K + 2, B], F32, name="terms")
         cons_w_sb = held.tile([P, B], F32, name="cons_w_sb")
         windows = [held.tile([P, S], F32, name=f"window{b}") for b in range(B)]
 
         nc.sync.dma_start(state_w_sb[:], state_w.rearrange("(p b) k -> p b k", b=B))
         nc.scalar.dma_start(state_sb[:], state.rearrange("o k -> (o k)").partition_broadcast(P))
-        nc.sync.dma_start(cons_b_sb[:], cons_b.rearrange("(p b) o -> p (b o)", b=B))
-        nc.scalar.dma_start(state_b_sb[:], state_b.rearrange("(p b) o -> p (b o)", b=B))
+        nc.sync.dma_start(terms[:, K, :], cons_b.rearrange("(p b) o -> p (b o)", b=B))
+        nc.scalar.dma_start(terms[:, K + 1, :], state_b.rearrange("(p b) o -> p (b o)", b=B))
         nc.sync.dma_start(cons_w_sb[:], cons_w.rearrange("(p b) o -> p (b o)", b=B))
         nc.scalar.dma_start(cons_sb[:], cons.rearrange("o n -> (o n)").partition_broadcast(P))
         nc.sync.dma_start(offsets[:], offs)
         for b in range(B):
             nc.sync.dma_start(windows[b][:], emb_blocks[b])
 
-        products = held.tile([P, B, K], F32, name="products")
         nc.vector.tensor_tensor(
-            products[:], state_w_sb[:], state_sb[:].unsqueeze(1).to_broadcast([P, B, K]), MULT
+            terms[:, 0:K, :],
+            state_w_sb[:].rearrange("p b k -> p k b"),
+            state_sb[:].unsqueeze(2).to_broadcast([P, K, B]),
+            MULT,
         )
         bias = held.tile([P, B], F32, name="bias")
-        nc.vector.tensor_reduce(bias[:], products[:], axis=mybir.AxisListType.X, op=ADD)
-        nc.vector.tensor_tensor(bias[:], bias[:], cons_b_sb[:], ADD)
-        nc.vector.tensor_tensor(bias[:], bias[:], state_b_sb[:], ADD)
+        nc.vector.tensor_reduce(
+            bias[:], terms[:].rearrange("p t b -> p b t"), axis=mybir.AxisListType.X, op=ADD
+        )
 
         others = []
         for b in range(B):

@@ -32,7 +32,7 @@ def tile_allostericmessagepassingencoder_kernel(
         nc.sync.dma_start(terms[:, K, :], cons_b.rearrange("(p b) o -> p (b o)", b=B))
         nc.scalar.dma_start(terms[:, K + 1, :], state_b.rearrange("(p b) o -> p (b o)", b=B))
         nc.sync.dma_start(cons_w_sb[:], cons_w.rearrange("(p b) o -> p (b o)", b=B))
-        nc.scalar.dma_start(cons_sb[:], cons.rearrange("o n -> (o n)").partition_broadcast(P))
+        nc.sync.dma_start(cons_sb[:], cons.rearrange("o n -> (o n)").partition_broadcast(P))
         nc.sync.dma_start(offsets[:], offs)
         for b in range(B):
             nc.sync.dma_start(windows[b][:], emb_blocks[b])

@@ -28,11 +28,11 @@ def tile_allostericmessagepassingencoder_kernel(
         windows = [held.tile([P, S], F32, name=f"window{b}") for b in range(B)]
 
         nc.sync.dma_start(state_w_sb[:], state_w.rearrange("(p b) k -> p b k", b=B))
+        nc.sync.dma_start(cons_sb[:], cons.rearrange("o n -> (o n)").partition_broadcast(P))
         nc.scalar.dma_start(state_sb[:], state.rearrange("o k -> (o k)").partition_broadcast(P))
         nc.sync.dma_start(terms[:, K, :], cons_b.rearrange("(p b) o -> p (b o)", b=B))
         nc.scalar.dma_start(terms[:, K + 1, :], state_b.rearrange("(p b) o -> p (b o)", b=B))
         nc.sync.dma_start(cons_w_sb[:], cons_w.rearrange("(p b) o -> p (b o)", b=B))
-        nc.sync.dma_start(cons_sb[:], cons.rearrange("o n -> (o n)").partition_broadcast(P))
         nc.sync.dma_start(offsets[:], offs)
         for b in range(B):
             nc.sync.dma_start(windows[b][:], emb_blocks[b])

@@ -4,6 +4,7 @@ F32 = mybir.dt.float32
 U16 = mybir.dt.uint16
 ADD = mybir.AluOpType.add
 MULT = mybir.AluOpType.mult
+IDENTITY = mybir.ActivationFunctionType.Identity
 
 P = 128
 C, S, N, K = 512, 1024, 512, 3
@@ -37,6 +38,11 @@ def tile_allostericmessagepassingencoder_kernel(
         for b in range(B):
             nc.sync.dma_start(windows[b][:], emb_blocks[b])
 
+        zeros = held.tile([P, 1], F32, name="zeros")
+        warmed = held.tile([P, 1], F32, name="warmed")
+        nc.gpsimd.memset(zeros[:], 0.0)
+        nc.scalar.activation(warmed[:], zeros[:], IDENTITY)
+
         nc.vector.tensor_tensor(
             terms[:, 0:K, :],
             state_w_sb[:].rearrange("p b k -> p k b"),
@@ -51,9 +57,18 @@ def tile_allostericmessagepassingencoder_kernel(
         others = []
         for b in range(B):
             other = held.tile([P, N], F32, name=f"other{b}")
-            nc.vector.tensor_scalar(
-                other[:], cons_sb[:], cons_w_sb[:, b : b + 1], bias[:, b : b + 1], MULT, ADD
-            )
+            if b < B // 2:
+                nc.vector.tensor_scalar(
+                    other[:], cons_sb[:], cons_w_sb[:, b : b + 1], bias[:, b : b + 1], MULT, ADD
+                )
+            else:
+                nc.scalar.activation(
+                    other[:],
+                    cons_sb[:],
+                    IDENTITY,
+                    bias=bias[:, b : b + 1],
+                    scale=cons_w_sb[:, b : b + 1],
+                )
             others.append(other)
 
         for b in range(B):

@@ -57,7 +57,7 @@ def tile_allostericmessagepassingencoder_kernel(
         others = []
         for b in range(B):
             other = held.tile([P, N], F32, name=f"other{b}")
-            if b < B // 2:
+            if b == 0:
                 nc.vector.tensor_scalar(
                     other[:], cons_sb[:], cons_w_sb[:, b : b + 1], bias[:, b : b + 1], MULT, ADD
                 )

import concourse.mybir as mybir

F32 = mybir.dt.float32
U16 = mybir.dt.uint16
ADD = mybir.AluOpType.add
MULT = mybir.AluOpType.mult
IDENTITY = mybir.ActivationFunctionType.Identity

P = 128
C, S, N, K = 512, 1024, 512, 3
B = C // P


def tile_allostericmessagepassingencoder_kernel(
    tc, emb, cons, cons_w, cons_b, state, state_w, state_b, offs, out
):
    nc = tc.nc

    emb_blocks = emb.rearrange("(p b) s -> b p s", b=B)
    out_blocks = out.rearrange("(p b) n -> b p n", b=B)

    with tc.tile_pool(name="held", bufs=1) as held:
        offsets = held.tile([P, N // 16], U16, name="offsets")
        state_w_sb = held.tile([P, B, K], F32, name="state_w_sb")
        state_sb = held.tile([P, K], F32, name="state_sb")
        cons_sb = held.tile([P, N], F32, name="cons_sb")
        terms = held.tile([P, K + 2, B], F32, name="terms")
        cons_w_sb = held.tile([P, B], F32, name="cons_w_sb")
        windows = [held.tile([P, S], F32, name=f"window{b}") for b in range(B)]

        nc.sync.dma_start(state_w_sb[:], state_w.rearrange("(p b) k -> p b k", b=B))
        nc.sync.dma_start(cons_sb[:], cons.rearrange("o n -> (o n)").partition_broadcast(P))
        nc.scalar.dma_start(state_sb[:], state.rearrange("o k -> (o k)").partition_broadcast(P))
        nc.sync.dma_start(terms[:, K, :], cons_b.rearrange("(p b) o -> p (b o)", b=B))
        nc.scalar.dma_start(terms[:, K + 1, :], state_b.rearrange("(p b) o -> p (b o)", b=B))
        nc.sync.dma_start(cons_w_sb[:], cons_w.rearrange("(p b) o -> p (b o)", b=B))
        nc.sync.dma_start(offsets[:], offs)
        for b in range(B):
            nc.sync.dma_start(windows[b][:], emb_blocks[b])

        zeros = held.tile([P, 1], F32, name="zeros")
        warmed = held.tile([P, 1], F32, name="warmed")
        nc.gpsimd.memset(zeros[:], 0.0)
        nc.scalar.activation(warmed[:], zeros[:], IDENTITY)

        nc.vector.tensor_tensor(
            terms[:, 0:K, :],
            state_w_sb[:].rearrange("p b k -> p k b"),
            state_sb[:].unsqueeze(2).to_broadcast([P, K, B]),
            MULT,
        )
        bias = held.tile([P, B], F32, name="bias")
        nc.vector.tensor_reduce(
            bias[:], terms[:].rearrange("p t b -> p b t"), axis=mybir.AxisListType.X, op=ADD
        )

        others = []
        for b in range(B):
            other = held.tile([P, N], F32, name=f"other{b}")
            if b == 0:
                nc.vector.tensor_scalar(
                    other[:], cons_sb[:], cons_w_sb[:, b : b + 1], bias[:, b : b + 1], MULT, ADD
                )
            else:
                nc.scalar.activation(
                    other[:],
                    cons_sb[:],
                    IDENTITY,
                    bias=bias[:, b : b + 1],
                    scale=cons_w_sb[:, b : b + 1],
                )
            others.append(other)

        for b in range(B):
            result = held.tile([P, N], F32, name=f"result{b}")
            pieces = 2 if b == B - 1 else 1
            n = N // pieces
            for j in range(0, N, n):
                nc.vector.tensor_tensor(
                    result[:, j : j + n],
                    windows[b][:].indirect(offsets[:, j // 16 : (j + n) // 16]),
                    others[b][:, j : j + n],
                    ADD,
                )
                nc.sync.dma_start(out_blocks[b][:, j : j + n], result[:, j : j + n])
